import numpy as np
import ml_dtypes

BF16 = ml_dtypes.bfloat16


def bf(x):
    return np.asarray(x, np.float32).astype(BF16)


def f32(x):
    return np.asarray(x, np.float32)


def f64(x):
    return np.asarray(x).astype(np.float64)


def striped(idx):
    return np.tile(idx.reshape(-1, 16).T, (8, 1))


C, S, N = 256, 2048, 2048
SCALE = np.sqrt(C)


def setup_inputs():
    return {"emb": f32(0.25 * np.random.standard_normal((C, S))), "pos": f32(np.random.standard_normal((C, N))), "offs": striped(np.random.permutation(np.tile(np.arange(S), 2))[:N])}


def reference(emb, pos, offs):
    idx = offs[:16].T.reshape(-1)
    return f64(emb)[:, idx] * SCALE + f64(pos)

@@ -1,0 +1,41 @@
+import concourse.mybir as mybir
+
+F32 = mybir.dt.float32
+U16 = mybir.dt.uint16
+ADD = mybir.AluOpType.add
+
+P = 128
+C, S, N = 256, 2048, 2048
+BLOCKS = C // P
+SCALE = 16.0
+PIECE = 512
+PIECES = N // PIECE
+PER_COLUMN = 16
+
+
+def tile_transformerencoder_kernel(tc, emb, pos, offs, out):
+    nc = tc.nc
+    with (
+        tc.tile_pool(name="held", bufs=1) as held,
+        tc.tile_pool(name="work", bufs=4) as work,
+    ):
+        offsets = held.tile([P, N // PER_COLUMN], U16, name="offsets")
+        nc.sync.dma_start(offsets[:], offs)
+
+        for b in range(BLOCKS):
+            rows = slice(b * P, (b + 1) * P)
+            table = held.tile([P, S], F32, name=f"table{b}")
+            nc.sync.dma_start(table[:], emb[rows, :])
+
+            for k in range(PIECES):
+                cols = slice(k * PIECE, (k + 1) * PIECE)
+                listed = offsets[:, k * PIECE // PER_COLUMN : (k + 1) * PIECE // PER_COLUMN]
+
+                place = work.tile([P, PIECE], F32, name="place")
+                nc.sync.dma_start(place[:], pos[rows, cols])
+                nc.scalar.mul(place[:], place[:], 1.0 / SCALE)
+
+                summed = work.tile([P, PIECE], F32, name="summed")
+                nc.vector.tensor_tensor(summed[:], table[:].indirect(listed), place[:], ADD)
+                nc.scalar.mul(summed[:], summed[:], SCALE)
+                nc.sync.dma_start(out[rows, cols], summed[:])

@@ -11,31 +11,46 @@ SCALE = 16.0
 PIECE = 512
 PIECES = N // PIECE
 PER_COLUMN = 16
+AHEAD = 3
 
 
 def tile_transformerencoder_kernel(tc, emb, pos, offs, out):
     nc = tc.nc
-    with (
-        tc.tile_pool(name="held", bufs=1) as held,
-        tc.tile_pool(name="work", bufs=4) as work,
-    ):
+    steps = [(b, k) for b in range(BLOCKS) for k in range(PIECES)]
+
+    with tc.tile_pool(name="held", bufs=1) as held:
         offsets = held.tile([P, N // PER_COLUMN], U16, name="offsets")
+        tables = [held.tile([P, S], F32, name=f"table{b}") for b in range(BLOCKS)]
+        places = {(b, k): held.tile([P, PIECE], F32, name=f"place{b}_{k}") for b, k in steps}
+        sums = {(b, k): held.tile([P, PIECE], F32, name=f"sum{b}_{k}") for b, k in steps}
+
+        def rows(b):
+            return slice(b * P, (b + 1) * P)
+
+        def cols(k):
+            return slice(k * PIECE, (k + 1) * PIECE)
+
+        def load_place(b, k):
+            nc.sync.dma_start(places[b, k][:], pos[rows(b), cols(k)])
+
+        def shrink_place(b, k):
+            nc.scalar.mul(places[b, k][:], places[b, k][:], 1.0 / SCALE)
+
         nc.sync.dma_start(offsets[:], offs)
-
         for b in range(BLOCKS):
-            rows = slice(b * P, (b + 1) * P)
-            table = held.tile([P, S], F32, name=f"table{b}")
-            nc.sync.dma_start(table[:], emb[rows, :])
+            load_place(b, 0)
+            nc.sync.dma_start(tables[b][:], emb[rows(b), :])
+            for k in range(1, PIECES):
+                load_place(b, k)
 
-            for k in range(PIECES):
-                cols = slice(k * PIECE, (k + 1) * PIECE)
-                listed = offsets[:, k * PIECE // PER_COLUMN : (k + 1) * PIECE // PER_COLUMN]
+        for b, k in steps[:AHEAD]:
+            shrink_place(b, k)
 
-                place = work.tile([P, PIECE], F32, name="place")
-                nc.sync.dma_start(place[:], pos[rows, cols])
-                nc.scalar.mul(place[:], place[:], 1.0 / SCALE)
-
-                summed = work.tile([P, PIECE], F32, name="summed")
-                nc.vector.tensor_tensor(summed[:], table[:].indirect(listed), place[:], ADD)
-                nc.scalar.mul(summed[:], summed[:], SCALE)
-                nc.sync.dma_start(out[rows, cols], summed[:])
+        for i, (b, k) in enumerate(steps):
+            listed = offsets[:, k * PIECE // PER_COLUMN : (k + 1) * PIECE // PER_COLUMN]
+            summed = sums[b, k]
+            nc.vector.tensor_tensor(summed[:], tables[b][:].indirect(listed), places[b, k][:], ADD)
+            nc.scalar.mul(summed[:], summed[:], SCALE)
+            nc.sync.dma_start(out[rows(b), cols(k)], summed[:])
+            if i + AHEAD < len(steps):
+                shrink_place(*steps[i + AHEAD])

@@ -8,49 +8,58 @@ P = 128
 C, S, N = 256, 2048, 2048
 BLOCKS = C // P
 SCALE = 16.0
-PIECE = 512
-PIECES = N // PIECE
 PER_COLUMN = 16
 AHEAD = 3
+
+WIDTHS = ((512, 512, 512, 512), (512, 512, 512, 256, 128, 128))
+assert len(WIDTHS) == BLOCKS and all(sum(widths) == N for widths in WIDTHS)
 
 
 def tile_transformerencoder_kernel(tc, emb, pos, offs, out):
     nc = tc.nc
-    steps = [(b, k) for b in range(BLOCKS) for k in range(PIECES)]
+
+    pieces = [
+        (b, sum(widths[:k]), widths[k]) for b, widths in enumerate(WIDTHS) for k in range(len(widths))
+    ]
 
     with tc.tile_pool(name="held", bufs=1) as held:
         offsets = held.tile([P, N // PER_COLUMN], U16, name="offsets")
         tables = [held.tile([P, S], F32, name=f"table{b}") for b in range(BLOCKS)]
-        places = {(b, k): held.tile([P, PIECE], F32, name=f"place{b}_{k}") for b, k in steps}
-        sums = {(b, k): held.tile([P, PIECE], F32, name=f"sum{b}_{k}") for b, k in steps}
+        places = {
+            (b, first, width): held.tile([P, width], F32, name=f"place{b}_{first}")
+            for b, first, width in pieces
+        }
+        sums = {
+            (b, first, width): held.tile([P, width], F32, name=f"sum{b}_{first}")
+            for b, first, width in pieces
+        }
 
         def rows(b):
             return slice(b * P, (b + 1) * P)
 
-        def cols(k):
-            return slice(k * PIECE, (k + 1) * PIECE)
+        def load_place(piece):
+            b, first, width = piece
+            nc.sync.dma_start(places[piece][:], pos[rows(b), first : first + width])
 
-        def load_place(b, k):
-            nc.sync.dma_start(places[b, k][:], pos[rows(b), cols(k)])
-
-        def shrink_place(b, k):
-            nc.scalar.mul(places[b, k][:], places[b, k][:], 1.0 / SCALE)
+        def shrink_place(piece):
+            nc.scalar.mul(places[piece][:], places[piece][:], 1.0 / SCALE)
 
         nc.sync.dma_start(offsets[:], offs)
-        for b in range(BLOCKS):
-            load_place(b, 0)
-            nc.sync.dma_start(tables[b][:], emb[rows(b), :])
-            for k in range(1, PIECES):
-                load_place(b, k)
+        for piece in pieces:
+            b, first, width = piece
+            load_place(piece)
+            if first == 0:
+                nc.sync.dma_start(tables[b][:], emb[rows(b), :])
 
-        for b, k in steps[:AHEAD]:
-            shrink_place(b, k)
+        for piece in pieces[:AHEAD]:
+            shrink_place(piece)
 
-        for i, (b, k) in enumerate(steps):
-            listed = offsets[:, k * PIECE // PER_COLUMN : (k + 1) * PIECE // PER_COLUMN]
-            summed = sums[b, k]
-            nc.vector.tensor_tensor(summed[:], tables[b][:].indirect(listed), places[b, k][:], ADD)
+        for i, piece in enumerate(pieces):
+            b, first, width = piece
+            listed = offsets[:, first // PER_COLUMN : (first + width) // PER_COLUMN]
+            summed = sums[piece]
+            nc.vector.tensor_tensor(summed[:], tables[b][:].indirect(listed), places[piece][:], ADD)
             nc.scalar.mul(summed[:], summed[:], SCALE)
-            nc.sync.dma_start(out[rows(b), cols(k)], summed[:])
-            if i + AHEAD < len(steps):
-                shrink_place(*steps[i + AHEAD])
+            nc.sync.dma_start(out[rows(b), first : first + width], summed[:])
+            if i + AHEAD < len(pieces):
+                shrink_place(pieces[i + AHEAD])

@@ -9,7 +9,6 @@ C, S, N = 256, 2048, 2048
 BLOCKS = C // P
 SCALE = 16.0
 PER_COLUMN = 16
-AHEAD = 3
 
 WIDTHS = ((512, 512, 512, 512), (512, 512, 512, 256, 128, 128))
 assert len(WIDTHS) == BLOCKS and all(sum(widths) == N for widths in WIDTHS)
@@ -21,6 +20,9 @@ def tile_transformerencoder_kernel(tc, emb, pos, offs, out):
     pieces = [
         (b, sum(widths[:k]), widths[k]) for b, widths in enumerate(WIDTHS) for k in range(len(widths))
     ]
+
+    def rows(b):
+        return slice(b * P, (b + 1) * P)
 
     with tc.tile_pool(name="held", bufs=1) as held:
         offsets = held.tile([P, N // PER_COLUMN], U16, name="offsets")
@@ -34,32 +36,20 @@ def tile_transformerencoder_kernel(tc, emb, pos, offs, out):
             for b, first, width in pieces
         }
 
-        def rows(b):
-            return slice(b * P, (b + 1) * P)
-
-        def load_place(piece):
-            b, first, width = piece
-            nc.sync.dma_start(places[piece][:], pos[rows(b), first : first + width])
-
-        def shrink_place(piece):
-            nc.scalar.mul(places[piece][:], places[piece][:], 1.0 / SCALE)
-
         nc.sync.dma_start(offsets[:], offs)
         for piece in pieces:
             b, first, width = piece
-            load_place(piece)
+            nc.sync.dma_start(places[piece][:], pos[rows(b), first : first + width])
             if first == 0:
                 nc.sync.dma_start(tables[b][:], emb[rows(b), :])
 
-        for piece in pieces[:AHEAD]:
-            shrink_place(piece)
+        for piece in pieces:
+            nc.scalar.mul(places[piece][:], places[piece][:], 1.0 / SCALE)
 
-        for i, piece in enumerate(pieces):
+        for piece in pieces:
             b, first, width = piece
             listed = offsets[:, first // PER_COLUMN : (first + width) // PER_COLUMN]
             summed = sums[piece]
             nc.vector.tensor_tensor(summed[:], tables[b][:].indirect(listed), places[piece][:], ADD)
             nc.scalar.mul(summed[:], summed[:], SCALE)
             nc.sync.dma_start(out[rows(b), first : first + width], summed[:])
-            if i + AHEAD < len(pieces):
-                shrink_place(pieces[i + AHEAD])

@@ -10,6 +10,8 @@ BLOCKS = C // P
 SCALE = 16.0
 PER_COLUMN = 16
 
+CHUNK = 512
+
 WIDTHS = ((512, 512, 512, 512), (512, 512, 512, 256, 128, 128))
 assert len(WIDTHS) == BLOCKS and all(sum(widths) == N for widths in WIDTHS)
 
@@ -37,19 +39,24 @@ def tile_transformerencoder_kernel(tc, emb, pos, offs, out):
         }
 
         nc.sync.dma_start(offsets[:], offs)
-        for piece in pieces:
-            b, first, width = piece
-            nc.sync.dma_start(places[piece][:], pos[rows(b), first : first + width])
-            if first == 0:
-                nc.sync.dma_start(tables[b][:], emb[rows(b), :])
+        for b in range(BLOCKS):
+            for word in range(0, S, CHUNK):
+                nc.sync.dma_start(tables[b][:, word : word + CHUNK], emb[rows(b), word : word + CHUNK])
+            for piece in pieces:
+                if piece[0] == b:
+                    first, width = piece[1:]
+                    nc.sync.dma_start(places[piece][:], pos[rows(b), first : first + width])
 
-        for piece in pieces:
-            nc.scalar.mul(places[piece][:], places[piece][:], 1.0 / SCALE)
+        for word in range(0, S, CHUNK):
+            chunk = tables[0][:, word : word + CHUNK]
+            nc.vector.tensor_scalar_mul(chunk, chunk, SCALE)
+        for word in range(0, S, CHUNK):
+            chunk = tables[1][:, word : word + CHUNK]
+            nc.scalar.mul(chunk, chunk, SCALE)
 
         for piece in pieces:
             b, first, width = piece
             listed = offsets[:, first // PER_COLUMN : (first + width) // PER_COLUMN]
             summed = sums[piece]
             nc.vector.tensor_tensor(summed[:], tables[b][:].indirect(listed), places[piece][:], ADD)
-            nc.scalar.mul(summed[:], summed[:], SCALE)
             nc.sync.dma_start(out[rows(b), first : first + width], summed[:])

@@ -12,7 +12,7 @@ PER_COLUMN = 16
 
 CHUNK = 512
 
-WIDTHS = ((512, 512, 512, 512), (512, 512, 512, 256, 128, 128))
+WIDTHS = ((256, 512, 1280), (512, 768, 384, 256, 128))
 assert len(WIDTHS) == BLOCKS and all(sum(widths) == N for widths in WIDTHS)
 
 

@@ -10,18 +10,27 @@ BLOCKS = C // P
 SCALE = 16.0
 PER_COLUMN = 16
 
-CHUNK = 512
 
-WIDTHS = ((256, 512, 1280), (512, 768, 384, 256, 128))
-assert len(WIDTHS) == BLOCKS and all(sum(widths) == N for widths in WIDTHS)
+TABLE_CHUNKS = ((1024, 512, 512), (512, 512, 512, 512))
+
+POS_LOADS = ((256, 512, 1280), (512, 768, 768))
+
+LOOKUPS = ((256, 512, 1280), (512, 768, 384, 256, 128))
+
+STORES = ((2048,), (512, 768, 384, 256, 128))
+
+assert S == N and all(
+    len(cuts) == BLOCKS and all(sum(widths) == N for widths in cuts)
+    for cuts in (TABLE_CHUNKS, POS_LOADS, LOOKUPS, STORES)
+)
+
+
+def spans(widths):
+    return [(sum(widths[:k]), sum(widths[: k + 1])) for k in range(len(widths))]
 
 
 def tile_transformerencoder_kernel(tc, emb, pos, offs, out):
     nc = tc.nc
-
-    pieces = [
-        (b, sum(widths[:k]), widths[k]) for b, widths in enumerate(WIDTHS) for k in range(len(widths))
-    ]
 
     def rows(b):
         return slice(b * P, (b + 1) * P)
@@ -29,34 +38,30 @@ def tile_transformerencoder_kernel(tc, emb, pos, offs, out):
     with tc.tile_pool(name="held", bufs=1) as held:
         offsets = held.tile([P, N // PER_COLUMN], U16, name="offsets")
         tables = [held.tile([P, S], F32, name=f"table{b}") for b in range(BLOCKS)]
-        places = {
-            (b, first, width): held.tile([P, width], F32, name=f"place{b}_{first}")
-            for b, first, width in pieces
-        }
-        sums = {
-            (b, first, width): held.tile([P, width], F32, name=f"sum{b}_{first}")
-            for b, first, width in pieces
-        }
+        places = [held.tile([P, N], F32, name=f"places{b}") for b in range(BLOCKS)]
+        sums = [held.tile([P, N], F32, name=f"sums{b}") for b in range(BLOCKS)]
 
         nc.sync.dma_start(offsets[:], offs)
         for b in range(BLOCKS):
-            for word in range(0, S, CHUNK):
-                nc.sync.dma_start(tables[b][:, word : word + CHUNK], emb[rows(b), word : word + CHUNK])
-            for piece in pieces:
-                if piece[0] == b:
-                    first, width = piece[1:]
-                    nc.sync.dma_start(places[piece][:], pos[rows(b), first : first + width])
+            for first, end in spans(TABLE_CHUNKS[b]):
+                nc.sync.dma_start(tables[b][:, first:end], emb[rows(b), first:end])
+            for first, end in spans(POS_LOADS[b]):
+                nc.sync.dma_start(places[b][:, first:end], pos[rows(b), first:end])
 
-        for word in range(0, S, CHUNK):
-            chunk = tables[0][:, word : word + CHUNK]
-            nc.vector.tensor_scalar_mul(chunk, chunk, SCALE)
-        for word in range(0, S, CHUNK):
-            chunk = tables[1][:, word : word + CHUNK]
-            nc.scalar.mul(chunk, chunk, SCALE)
+        for first, end in spans(TABLE_CHUNKS[0]):
+            nc.vector.tensor_scalar_mul(tables[0][:, first:end], tables[0][:, first:end], SCALE)
+        for first, end in spans(TABLE_CHUNKS[1]):
+            nc.scalar.mul(tables[1][:, first:end], tables[1][:, first:end], SCALE)
 
-        for piece in pieces:
-            b, first, width = piece
-            listed = offsets[:, first // PER_COLUMN : (first + width) // PER_COLUMN]
-            summed = sums[piece]
-            nc.vector.tensor_tensor(summed[:], tables[b][:].indirect(listed), places[piece][:], ADD)
-            nc.sync.dma_start(out[rows(b), first : first + width], summed[:])
+        for b in range(BLOCKS):
+            stores = spans(STORES[b])
+            for first, end in spans(LOOKUPS[b]):
+                listed = offsets[:, first // PER_COLUMN : end // PER_COLUMN]
+                nc.vector.tensor_tensor(
+                    sums[b][:, first:end], tables[b][:].indirect(listed), places[b][:, first:end], ADD
+                )
+                for store_first, store_end in stores:
+                    if store_end == end:
+                        nc.sync.dma_start(
+                            out[rows(b), store_first:store_end], sums[b][:, store_first:store_end]
+                        )

@@ -13,9 +13,9 @@ PER_COLUMN = 16
 
 TABLE_CHUNKS = ((1024, 512, 512), (512, 512, 512, 512))
 
-POS_LOADS = ((256, 512, 1280), (512, 768, 768))
+POS_LOADS = ((256, 640, 1152), (512, 768, 768))
 
-LOOKUPS = ((256, 512, 1280), (512, 768, 384, 256, 128))
+LOOKUPS = ((256, 640, 1152), (512, 768, 384, 256, 128))
 
 STORES = ((2048,), (512, 768, 384, 256, 128))
 

import concourse.mybir as mybir

F32 = mybir.dt.float32
U16 = mybir.dt.uint16
ADD = mybir.AluOpType.add

P = 128
C, S, N = 256, 2048, 2048
BLOCKS = C // P
SCALE = 16.0
PER_COLUMN = 16


TABLE_CHUNKS = ((1024, 512, 512), (512, 512, 512, 512))

POS_LOADS = ((256, 640, 1152), (512, 768, 768))

LOOKUPS = ((256, 640, 1152), (512, 768, 384, 256, 128))

STORES = ((2048,), (512, 768, 384, 256, 128))

assert S == N and all(
    len(cuts) == BLOCKS and all(sum(widths) == N for widths in cuts)
    for cuts in (TABLE_CHUNKS, POS_LOADS, LOOKUPS, STORES)
)


def spans(widths):
    return [(sum(widths[:k]), sum(widths[: k + 1])) for k in range(len(widths))]


def tile_transformerencoder_kernel(tc, emb, pos, offs, out):
    nc = tc.nc

    def rows(b):
        return slice(b * P, (b + 1) * P)

    with tc.tile_pool(name="held", bufs=1) as held:
        offsets = held.tile([P, N // PER_COLUMN], U16, name="offsets")
        tables = [held.tile([P, S], F32, name=f"table{b}") for b in range(BLOCKS)]
        places = [held.tile([P, N], F32, name=f"places{b}") for b in range(BLOCKS)]
        sums = [held.tile([P, N], F32, name=f"sums{b}") for b in range(BLOCKS)]

        nc.sync.dma_start(offsets[:], offs)
        for b in range(BLOCKS):
            for first, end in spans(TABLE_CHUNKS[b]):
                nc.sync.dma_start(tables[b][:, first:end], emb[rows(b), first:end])
            for first, end in spans(POS_LOADS[b]):
                nc.sync.dma_start(places[b][:, first:end], pos[rows(b), first:end])

        for first, end in spans(TABLE_CHUNKS[0]):
            nc.vector.tensor_scalar_mul(tables[0][:, first:end], tables[0][:, first:end], SCALE)
        for first, end in spans(TABLE_CHUNKS[1]):
            nc.scalar.mul(tables[1][:, first:end], tables[1][:, first:end], SCALE)

        for b in range(BLOCKS):
            stores = spans(STORES[b])
            for first, end in spans(LOOKUPS[b]):
                listed = offsets[:, first // PER_COLUMN : end // PER_COLUMN]
                nc.vector.tensor_tensor(
                    sums[b][:, first:end], tables[b][:].indirect(listed), places[b][:, first:end], ADD
                )
                for store_first, store_end in stores:
                    if store_end == end:
                        nc.sync.dma_start(
                            out[rows(b), store_first:store_end], sums[b][:, store_first:store_end]
                        )
